import numpy as np
import ml_dtypes


def mxq(x, axis, fmt="e4m3"):
    dtype, down = {"e4m3": (ml_dtypes.float8_e4m3fn, 7), "e5m2": (ml_dtypes.float8_e5m2, 14)}[fmt]
    v = np.moveaxis(np.asarray(x, np.float32).astype(ml_dtypes.bfloat16).astype(np.float64), axis, -1)
    blocks = v.reshape(v.shape[:-1] + (-1, 32))
    amax = np.abs(blocks).max(-1, keepdims=True)
    byte = np.maximum(np.where(amax > 0, np.frexp(amax)[1] - 1 + 127, 0) - down, 1)
    scale = np.exp2(byte - 127.0)
    codes = (blocks / scale).astype(np.float32).astype(dtype).astype(np.float64)
    return np.moveaxis((codes * scale).reshape(v.shape), -1, axis)


WIDE = False


def mx_kscale(k):
    if not WIDE:
        return np.ones(k)
    levels = np.array([10, -10, 5, -5, 0])
    if k % 512:
        return np.exp2(np.random.permutation(np.resize(levels, k // 32))).repeat(32)
    a = np.empty((k // 512, 16))
    for p in range(k // 512):
        a[p, :8] = np.random.permutation(np.resize(levels, 8))
        for g in range(8):
            far = levels[np.abs(levels - a[p, g]) >= 10]
            a[p, g + 8] = far[np.random.randint(len(far))]
    return np.exp2(a.ravel()).repeat(32)


BF16 = ml_dtypes.bfloat16


def bf(x):
    return np.asarray(x, np.float32).astype(BF16)


def f64(x):
    return np.asarray(x).astype(np.float64)


B, N, E, H, C = 1, 1024, 2048, 8, 512
D = E // H


def decay_gammas():
    return 1.0 - np.exp(np.linspace(np.log(2.0 ** -5), np.log(2.0 ** -9), H))


def setup_inputs():
    t = mx_kscale(N)
    return {"q_rot": bf(np.random.standard_normal((B, H, N, D))),
            "k_scaled": bf(np.random.standard_normal((B, H, N, D)) / np.sqrt(D) * t[:, None]),
            "v": bf(np.random.standard_normal((B, H, N, D)) * 0.5 / t[:, None])}


def reference(q_rot, k_scaled, v):
    q, k = f64(q_rot), f64(k_scaled)
    vq = mxq(f64(v), 2, "e4m3")
    gam = decay_gammas()[:, None, None]
    out = []
    for i in range(N // C):
        lo, hi = i * C, (i + 1) * C
        dist = f64(np.arange(lo, hi))[:, None] - f64(np.arange(hi))[None, :]
        mask = gam ** np.where(dist < 0, np.inf, dist)
        sim = (q[:, :, lo:hi] @ k[:, :, :hi].transpose(0, 1, 3, 2)) * mask[None]
        out.append(mxq(sim, 3, "e4m3") @ vq[:, :, :hi])
    ret = np.concatenate(out, axis=2)
    return ret.transpose(0, 2, 1, 3).reshape(B, N, E)

@@ -1,0 +1,221 @@
+import math
+from contextlib import ExitStack
+
+import concourse.mybir as mybir
+from concourse.masks import make_identity
+
+BF16 = mybir.dt.bfloat16
+F32 = mybir.dt.float32
+U32 = mybir.dt.uint32
+U8 = mybir.dt.uint8
+FP8X4 = mybir.dt.float8_e4m3fn_x4
+
+H = 8
+N = 1024
+D = 256
+P = 128
+PACK = 4
+PAIR = 2
+CHUNK = PACK * P
+CHUNKS = N // CHUNK
+
+BANKS = [(i, r, c) for i in range(CHUNKS) for r in range(PACK) for c in range(i + 1)]
+PAIRS = [(BANKS[b], BANKS[b + 1]) for b in range(0, len(BANKS), 2)]
+STEPS = len(PAIRS)
+MX_LAG = 2
+DECAY_AT = -3
+TURN_AT = {("k", 0): -2, ("q", 0): -2, ("q", 1): 0, ("k", 1): 1}
+REGROUP_AT = [0, 2]
+FIRST_STEP = min([DECAY_AT] + list(TURN_AT.values()) + REGROUP_AT)
+FAR = 1.0e6
+SPAN = N + PACK
+
+FLOPS = 2 * 2 * H * D * len(BANKS) * P * CHUNK
+
+
+def log_decay(h):
+    first, last = math.log(2.0 ** -5), math.log(2.0 ** -9)
+    return math.log(1.0 - math.exp(first + (last - first) * h / (H - 1)))
+
+
+def tile_multiscaleretention_pb_kernel(tc, q_rot, k_scaled, v, out):
+    nc = tc.nc
+    out_rows = out[0].rearrange("(i p r) e -> i p r e", p=P, r=PACK)
+
+    with ExitStack() as ctx:
+        const = ctx.enter_context(tc.tile_pool(name="const", bufs=1))
+        raw = ctx.enter_context(tc.tile_pool(name="raw", bufs=3))
+        turned_pool = ctx.enter_context(tc.tile_pool(name="turned_pool", bufs=2))
+        decays = ctx.enter_context(tc.tile_pool(name="decays", bufs=2))
+        values_in = ctx.enter_context(tc.tile_pool(name="values_in", bufs=2 * CHUNKS))
+        packed = ctx.enter_context(tc.tile_pool(name="packed", bufs=4))
+        results = ctx.enter_context(tc.tile_pool(name="results", bufs=4))
+        psum_turn = ctx.enter_context(tc.psum_pool(name="psum_turn", bufs=2))
+        psum_sim = ctx.enter_context(tc.psum_pool(name="psum_sim", bufs=4))
+        psum_ret = ctx.enter_context(tc.psum_pool(name="psum_ret", bufs=2))
+        ctx.enter_context(tc.manual_schedule())
+
+        identity = const.tile([P, P], F32)
+        make_identity(nc, identity[:])
+        distance = const.tile([P, SPAN], F32)
+        nc.gpsimd.iota(
+            distance[:], pattern=[[1, SPAN]], base=-(PACK - 1), channel_multiplier=-PACK,
+            allow_small_or_imprecise_dtypes=True,
+        )
+        near_part = distance[:, 0:CHUNK]
+        nc.vector.scalar_tensor_tensor(
+            out=near_part,
+            in0=near_part,
+            scalar=-FAR,
+            in1=near_part,
+            op0=mybir.AluOpType.mult,
+            op1=mybir.AluOpType.max,
+        )
+
+        raws = {}
+        turned = {}
+        decay = {}
+        v_grouped, v_codes, v_scales = {}, {}, {}
+        sim = {}
+        grouped, codes, scales = {}, {}, {}
+        ret = {}
+
+        def load(h):
+            sources = {"q": q_rot, "k": k_scaled, "v": v}
+            for what in ("q", "k", "v"):
+                raws[(h, what)] = raw.tile([P, CHUNKS, PACK, D], BF16, name=what + "_raw")
+            for what, c in (("k", 0), ("q", 0), ("q", 1), ("v", 0), ("k", 1), ("v", 1)):
+                rows = sources[what][0, h, c * CHUNK : (c + 1) * CHUNK, :]
+                nc.sync.dma_start(
+                    out=raws[(h, what)][:, c], in_=rows.rearrange("(p t) d -> p t d", t=PACK)
+                )
+
+        def turn(h, what, c):
+            if c == 0:
+                turned[(h, what)] = turned_pool.tile(
+                    [P, CHUNKS, PACK, P, PAIR], BF16, name=what + "_turned"
+                )
+            bank = psum_turn.tile([P, PACK, P], F32, name="turn_bank")
+            for t in range(PACK):
+                nc.tensor.transpose(
+                    bank[:, t, :], raws[(h, what)][:, c, t, :].bitcast(F32), identity[:]
+                )
+            words = turned[(h, what)][:, c].rearrange("w t p e -> w (t p e)").bitcast(F32)
+            nc.scalar.copy(out=words, in_=bank[:].rearrange("w t p -> w (t p)"))
+
+        def make_decay(h):
+            decay[h] = decays.tile([P, SPAN], F32, name="decay")
+            nc.scalar.activation(
+                out=decay[h][:],
+                in_=distance[:],
+                func=mybir.ActivationFunctionType.Exp,
+                scale=log_decay(h),
+            )
+
+        def regroup_values(h, c):
+            v_grouped[(h, c)] = values_in.tile([P, D, PACK], BF16, name="v_grouped", align_bytes=64)
+            nc.scalar.copy(
+                out=v_grouped[(h, c)][:].rearrange("p (b i) t -> p b t i", i=4),
+                in_=raws[(h, "v")][:, c].rearrange("p t (b i) -> p b t i", i=4),
+            )
+
+        def quantise_values(h, c):
+            v_codes[(h, c)] = values_in.tile([P, D], U32, name="v_codes", align_bytes=64)
+            v_scales[(h, c)] = values_in.tile([P, D], U8, name="v_scales", align_bytes=64)
+            nc.vector.quantize_mx(
+                out=v_codes[(h, c)][:].bitcast(FP8X4),
+                scales=v_scales[(h, c)][:],
+                in_=v_grouped[(h, c)][:].rearrange("p d t -> p (d t)"),
+            )
+
+        def scores(h, k, b):
+            i, r, c = PAIRS[k][b]
+            sums = psum_sim.tile([P, PACK, P], F32, name="sums")
+            sim[(h, k, b)] = sums
+            for t in range(PACK):
+                for e in range(PAIR):
+                    nc.tensor.matmul(
+                        sums[:, t, :],
+                        lhsT=turned[(h, "k")][:, c, t, :, e],
+                        rhs=turned[(h, "q")][:, i, r, :, e],
+                        start=(e == 0),
+                        stop=(e == PAIR - 1),
+                    )
+
+        def apply_decay(h, k, b):
+            i, r, c = PAIRS[k][b]
+            if b == 0:
+                grouped[(h, k)] = packed.tile([P, 2, P, PACK], BF16, name="grouped", align_bytes=64)
+            first = CHUNK * (i - c) + r
+            window = decay[h][:, first : first + CHUNK].rearrange("p (m z) -> p m z", z=PACK)
+            nc.vector.tensor_tensor(
+                out=grouped[(h, k)][:, b],
+                in0=sim[(h, k, b)][:].rearrange("p t m -> p m t"),
+                in1=window[:, :, ::-1],
+                op=mybir.AluOpType.mult,
+            )
+
+        def quantise(h, k):
+            codes[(h, k)] = packed.tile([P, 2, P], U32, name="codes", align_bytes=64)
+            scales[(h, k)] = packed.tile([P, 2, P], U8, name="scales", align_bytes=64)
+            nc.vector.quantize_mx(
+                out=codes[(h, k)][:].rearrange("p b m -> p (b m)").bitcast(FP8X4),
+                scales=scales[(h, k)][:].rearrange("p b m -> p (b m)"),
+                in_=grouped[(h, k)][:].rearrange("p b m t -> p (b m t)"),
+            )
+
+        def weigh_values(h, k):
+            for b, (i, r, c) in enumerate(PAIRS[k]):
+                if r % 2 == 0 and c == 0:
+                    ret["now"] = psum_ret.tile([P, 2, D], F32, name="ret_bank")
+                nc.tensor.matmul_mx(
+                    out=ret["now"][:, r % 2, :],
+                    lhsT=codes[(h, k)][:, b, :].bitcast(FP8X4),
+                    lhsT_scale=scales[(h, k)][:, b, :],
+                    rhs=v_codes[(h, c)][:].bitcast(FP8X4),
+                    rhs_scale=v_scales[(h, c)][:],
+                    start=(c == 0),
+                    stop=(c == i),
+                )
+                if r % 2 == 1 and c == i:
+                    result = results.tile([P, 2, D], F32, name="result")
+                    nc.scalar.copy(out=result[:], in_=ret["now"][:])
+                    nc.sync.dma_start(
+                        out=out_rows[i, :, r - 1 : r + 1, h * D : (h + 1) * D], in_=result[:]
+                    )
+
+        load(0)
+        load(1)
+        last_step = H * STEPS - 1
+        for g in range(FIRST_STEP, last_step + 1 + MX_LAG):
+            h, k = divmod(g, STEPS)
+            computing = 0 <= g <= last_step
+            near = [(head, g - head * STEPS) for head in (h, h + 1) if 0 <= head < H]
+            if computing and k == 0 and h + 2 < H:
+                load(h + 2)
+            for head, step in near:
+                if step == DECAY_AT:
+                    make_decay(head)
+            if computing:
+                scores(h, k, 0)
+            for head, step in near:
+                for (what, c), at in TURN_AT.items():
+                    if step == at:
+                        turn(head, what, c)
+            if computing:
+                scores(h, k, 1)
+                apply_decay(h, k, 0)
+            if 0 <= g - 1 <= last_step:
+                quantise(*divmod(g - 1, STEPS))
+            if computing:
+                apply_decay(h, k, 1)
+            for head, step in near:
+                for c in range(CHUNKS):
+                    if step == REGROUP_AT[c] + 1:
+                        quantise_values(head, c)
+            if 0 <= g - MX_LAG:
+                weigh_values(*divmod(g - MX_LAG, STEPS))
+            for head, step in near:
+                for c in range(CHUNKS):
+                    if step == REGROUP_AT[c]:
+                        regroup_values(head, c)

@@ -21,12 +21,12 @@ CHUNKS = N // CHUNK
 
 BANKS = [(i, r, c) for i in range(CHUNKS) for r in range(PACK) for c in range(i + 1)]
 PAIRS = [(BANKS[b], BANKS[b + 1]) for b in range(0, len(BANKS), 2)]
-STEPS = len(PAIRS)
+PER_ROUND = 2
 MX_LAG = 2
-DECAY_AT = -3
-TURN_AT = {("k", 0): -2, ("q", 0): -2, ("q", 1): 0, ("k", 1): 1}
-REGROUP_AT = [0, 2]
-FIRST_STEP = min([DECAY_AT] + list(TURN_AT.values()) + REGROUP_AT)
+ROUNDS = len(PAIRS) // PER_ROUND
+DECAY_AT = -1
+TURN_AT = {-1: (("k", 0), ("q", 0)), 0: (("q", 1), ("k", 1))}
+REGROUP_AT = [0, 1]
 FAR = 1.0e6
 SPAN = N + PACK
 
@@ -48,7 +48,7 @@ def tile_multiscaleretention_pb_kernel(tc, q_rot, k_scaled, v, out):
         turned_pool = ctx.enter_context(tc.tile_pool(name="turned_pool", bufs=2))
         decays = ctx.enter_context(tc.tile_pool(name="decays", bufs=2))
         values_in = ctx.enter_context(tc.tile_pool(name="values_in", bufs=2 * CHUNKS))
-        packed = ctx.enter_context(tc.tile_pool(name="packed", bufs=4))
+        packed = ctx.enter_context(tc.tile_pool(name="packed", bufs=7))
         results = ctx.enter_context(tc.tile_pool(name="results", bufs=4))
         psum_turn = ctx.enter_context(tc.psum_pool(name="psum_turn", bufs=2))
         psum_sim = ctx.enter_context(tc.psum_pool(name="psum_sim", bufs=4))
@@ -101,7 +101,8 @@ def tile_multiscaleretention_pb_kernel(tc, q_rot, k_scaled, v, out):
                     bank[:, t, :], raws[(h, what)][:, c, t, :].bitcast(F32), identity[:]
                 )
             words = turned[(h, what)][:, c].rearrange("w t p e -> w (t p e)").bitcast(F32)
-            nc.scalar.copy(out=words, in_=bank[:].rearrange("w t p -> w (t p)"))
+            copy = nc.vector.tensor_copy if (h, what, c) == (0, "q", 0) else nc.scalar.copy
+            copy(out=words, in_=bank[:].rearrange("w t p -> w (t p)"))
 
         def make_decay(h):
             decay[h] = decays.tile([P, SPAN], F32, name="decay")
@@ -186,36 +187,45 @@ def tile_multiscaleretention_pb_kernel(tc, q_rot, k_scaled, v, out):
 
         load(0)
         load(1)
-        last_step = H * STEPS - 1
-        for g in range(FIRST_STEP, last_step + 1 + MX_LAG):
-            h, k = divmod(g, STEPS)
-            computing = 0 <= g <= last_step
-            near = [(head, g - head * STEPS) for head in (h, h + 1) if 0 <= head < H]
+        last_round = H * ROUNDS - 1
+        for g in range(-1, last_round + MX_LAG + 1):
+            h, k = divmod(g, ROUNDS)
+            computing = 0 <= g <= last_round
+            first, second = PER_ROUND * k, PER_ROUND * k + 1
+            before = divmod(g - 1, ROUNDS)
+            near = [(head, g - head * ROUNDS) for head in (h, h + 1) if 0 <= head < H]
             if computing and k == 0 and h + 2 < H:
                 load(h + 2)
+            if computing:
+                scores(h, first, 0)
+                scores(h, first, 1)
+            for head, step in near:
+                for what, c in TURN_AT.get(step, ()):
+                    turn(head, what, c)
             for head, step in near:
                 if step == DECAY_AT:
                     make_decay(head)
             if computing:
-                scores(h, k, 0)
-            for head, step in near:
-                for (what, c), at in TURN_AT.items():
-                    if step == at:
-                        turn(head, what, c)
+                apply_decay(h, first, 0)
+            if 1 <= g <= last_round + 1:
+                quantise(before[0], PER_ROUND * before[1] + 1)
             if computing:
-                scores(h, k, 1)
-                apply_decay(h, k, 0)
-            if 0 <= g - 1 <= last_step:
-                quantise(*divmod(g - 1, STEPS))
-            if computing:
-                apply_decay(h, k, 1)
+                apply_decay(h, first, 1)
+                scores(h, second, 0)
+                scores(h, second, 1)
+                apply_decay(h, second, 0)
             for head, step in near:
                 for c in range(CHUNKS):
                     if step == REGROUP_AT[c] + 1:
                         quantise_values(head, c)
-            if 0 <= g - MX_LAG:
-                weigh_values(*divmod(g - MX_LAG, STEPS))
+            if computing:
+                quantise(h, first)
+                apply_decay(h, second, 1)
             for head, step in near:
                 for c in range(CHUNKS):
                     if step == REGROUP_AT[c]:
                         regroup_values(head, c)
+            if g >= MX_LAG:
+                h_due, k_due = divmod(g - MX_LAG, ROUNDS)
+                for k_in_round in range(PER_ROUND):
+                    weigh_values(h_due, PER_ROUND * k_due + k_in_round)

@@ -20,15 +20,16 @@ CHUNK = PACK * P
 CHUNKS = N // CHUNK
 
 BANKS = [(i, r, c) for i in range(CHUNKS) for r in range(PACK) for c in range(i + 1)]
-PAIRS = [(BANKS[b], BANKS[b + 1]) for b in range(0, len(BANKS), 2)]
-PER_ROUND = 2
+PER_ROUND = 4
 MX_LAG = 2
-ROUNDS = len(PAIRS) // PER_ROUND
+ROUNDS = len(BANKS) // PER_ROUND
 DECAY_AT = -1
 TURN_AT = {-1: (("k", 0), ("q", 0)), 0: (("q", 1), ("k", 1))}
-REGROUP_AT = [0, 1]
+REGROUP_AT = [-1, 0]
+QUANTISE_VALUES_AT = 1
 FAR = 1.0e6
 SPAN = N + PACK
+NEAR, FAR_OFF = slice(0, CHUNK + PACK), slice(CHUNK + PACK, SPAN)
 
 FLOPS = 2 * 2 * H * D * len(BANKS) * P * CHUNK
 
@@ -47,8 +48,8 @@ def tile_multiscaleretention_pb_kernel(tc, q_rot, k_scaled, v, out):
         raw = ctx.enter_context(tc.tile_pool(name="raw", bufs=3))
         turned_pool = ctx.enter_context(tc.tile_pool(name="turned_pool", bufs=2))
         decays = ctx.enter_context(tc.tile_pool(name="decays", bufs=2))
-        values_in = ctx.enter_context(tc.tile_pool(name="values_in", bufs=2 * CHUNKS))
-        packed = ctx.enter_context(tc.tile_pool(name="packed", bufs=7))
+        values_in = ctx.enter_context(tc.tile_pool(name="values_in", bufs=2))
+        packed = ctx.enter_context(tc.tile_pool(name="packed", bufs=4))
         results = ctx.enter_context(tc.tile_pool(name="results", bufs=4))
         psum_turn = ctx.enter_context(tc.psum_pool(name="psum_turn", bufs=2))
         psum_sim = ctx.enter_context(tc.psum_pool(name="psum_sim", bufs=4))
@@ -58,10 +59,12 @@ def tile_multiscaleretention_pb_kernel(tc, q_rot, k_scaled, v, out):
         identity = const.tile([P, P], F32)
         make_identity(nc, identity[:])
         distance = const.tile([P, SPAN], F32)
-        nc.gpsimd.iota(
-            distance[:], pattern=[[1, SPAN]], base=-(PACK - 1), channel_multiplier=-PACK,
-            allow_small_or_imprecise_dtypes=True,
-        )
+        for part in (NEAR, FAR_OFF):
+            nc.gpsimd.iota(
+                distance[:, part], pattern=[[1, part.stop - part.start]],
+                base=part.start - (PACK - 1), channel_multiplier=-PACK,
+                allow_small_or_imprecise_dtypes=True,
+            )
         near_part = distance[:, 0:CHUNK]
         nc.vector.scalar_tensor_tensor(
             out=near_part,
@@ -84,54 +87,64 @@ def tile_multiscaleretention_pb_kernel(tc, q_rot, k_scaled, v, out):
             sources = {"q": q_rot, "k": k_scaled, "v": v}
             for what in ("q", "k", "v"):
                 raws[(h, what)] = raw.tile([P, CHUNKS, PACK, D], BF16, name=what + "_raw")
-            for what, c in (("k", 0), ("q", 0), ("q", 1), ("v", 0), ("k", 1), ("v", 1)):
+            for what, c in (("q", 0), ("k", 0), ("v", 0), ("q", 1), ("k", 1), ("v", 1)):
                 rows = sources[what][0, h, c * CHUNK : (c + 1) * CHUNK, :]
-                nc.sync.dma_start(
-                    out=raws[(h, what)][:, c], in_=rows.rearrange("(p t) d -> p t d", t=PACK)
-                )
+                rows = rows.rearrange("(p t) d -> p t d", t=PACK)
+                halves = (slice(0, 2), slice(2, 4)) if (h, c) == (0, 0) and what != "v" else (slice(0, 4),)
+                for part in halves:
+                    nc.sync.dma_start(out=raws[(h, what)][:, c, part], in_=rows[:, part])
 
-        def turn(h, what, c):
-            if c == 0:
+        def turn(h, what, c, sets=range(PACK), bank_pool=psum_turn, copy=nc.scalar.copy):
+            if (h, what) not in turned:
                 turned[(h, what)] = turned_pool.tile(
                     [P, CHUNKS, PACK, P, PAIR], BF16, name=what + "_turned"
                 )
-            bank = psum_turn.tile([P, PACK, P], F32, name="turn_bank")
-            for t in range(PACK):
+            bank = bank_pool.tile([P, PACK, P], F32, name="bank")
+            for t in sets:
                 nc.tensor.transpose(
                     bank[:, t, :], raws[(h, what)][:, c, t, :].bitcast(F32), identity[:]
                 )
-            words = turned[(h, what)][:, c].rearrange("w t p e -> w (t p e)").bitcast(F32)
-            copy = nc.vector.tensor_copy if (h, what, c) == (0, "q", 0) else nc.scalar.copy
-            copy(out=words, in_=bank[:].rearrange("w t p -> w (t p)"))
+            part = slice(sets[0], sets[-1] + 1)
+            words = turned[(h, what)][:, c, part].rearrange("w t p e -> w (t p e)").bitcast(F32)
+            copy(out=words, in_=bank[:, part].rearrange("w t p -> w (t p)"))
+
+        def turn_first():
+            low, high = range(0, 2), range(2, 4)
+            turn(0, "q", 0, low, psum_sim, nc.vector.tensor_copy)
+            turn(0, "k", 0, low, psum_turn, nc.scalar.copy)
+            turn(0, "k", 0, high, psum_turn, nc.vector.tensor_copy)
+            turn(0, "q", 0, high, psum_sim, nc.scalar.copy)
 
         def make_decay(h):
             decay[h] = decays.tile([P, SPAN], F32, name="decay")
-            nc.scalar.activation(
-                out=decay[h][:],
-                in_=distance[:],
-                func=mybir.ActivationFunctionType.Exp,
-                scale=log_decay(h),
-            )
+            for part in (NEAR, FAR_OFF) if h == 0 else (slice(0, SPAN),):
+                nc.scalar.activation(
+                    out=decay[h][:, part],
+                    in_=distance[:, part],
+                    func=mybir.ActivationFunctionType.Exp,
+                    scale=log_decay(h),
+                )
 
         def regroup_values(h, c):
-            v_grouped[(h, c)] = values_in.tile([P, D, PACK], BF16, name="v_grouped", align_bytes=64)
+            if c == 0:
+                v_grouped[h] = values_in.tile([P, CHUNKS, D, PACK], BF16, name="v_grouped", align_bytes=64)
             nc.scalar.copy(
-                out=v_grouped[(h, c)][:].rearrange("p (b i) t -> p b t i", i=4),
+                out=v_grouped[h][:, c].rearrange("p (b i) t -> p b t i", i=4),
                 in_=raws[(h, "v")][:, c].rearrange("p t (b i) -> p b t i", i=4),
             )
 
-        def quantise_values(h, c):
-            v_codes[(h, c)] = values_in.tile([P, D], U32, name="v_codes", align_bytes=64)
-            v_scales[(h, c)] = values_in.tile([P, D], U8, name="v_scales", align_bytes=64)
+        def quantise_values(h):
+            v_codes[h] = values_in.tile([P, CHUNKS, D], U32, name="v_codes", align_bytes=64)
+            v_scales[h] = values_in.tile([P, CHUNKS, D], U8, name="v_scales", align_bytes=64)
             nc.vector.quantize_mx(
-                out=v_codes[(h, c)][:].bitcast(FP8X4),
-                scales=v_scales[(h, c)][:],
-                in_=v_grouped[(h, c)][:].rearrange("p d t -> p (d t)"),
+                out=v_codes[h][:].rearrange("p c d -> p (c d)").bitcast(FP8X4),
+                scales=v_scales[h][:].rearrange("p c d -> p (c d)"),
+                in_=v_grouped[h][:].rearrange("p c d t -> p (c d t)"),
             )
 
         def scores(h, k, b):
-            i, r, c = PAIRS[k][b]
-            sums = psum_sim.tile([P, PACK, P], F32, name="sums")
+            i, r, c = BANKS[PER_ROUND * k + b]
+            sums = psum_sim.tile([P, PACK, P], F32, name="bank")
             sim[(h, k, b)] = sums
             for t in range(PACK):
                 for e in range(PAIR):
@@ -144,9 +157,9 @@ def tile_multiscaleretention_pb_kernel(tc, q_rot, k_scaled, v, out):
                     )
 
         def apply_decay(h, k, b):
-            i, r, c = PAIRS[k][b]
+            i, r, c = BANKS[PER_ROUND * k + b]
             if b == 0:
-                grouped[(h, k)] = packed.tile([P, 2, P, PACK], BF16, name="grouped", align_bytes=64)
+                grouped[(h, k)] = packed.tile([P, PER_ROUND, P, PACK], BF16, name="grouped", align_bytes=64)
             first = CHUNK * (i - c) + r
             window = decay[h][:, first : first + CHUNK].rearrange("p (m z) -> p m z", z=PACK)
             nc.vector.tensor_tensor(
@@ -156,33 +169,38 @@ def tile_multiscaleretention_pb_kernel(tc, q_rot, k_scaled, v, out):
                 op=mybir.AluOpType.mult,
             )
 
-        def quantise(h, k):
-            codes[(h, k)] = packed.tile([P, 2, P], U32, name="codes", align_bytes=64)
-            scales[(h, k)] = packed.tile([P, 2, P], U8, name="scales", align_bytes=64)
+        def quantise(h, k, part):
+            if part.start == 0:
+                codes[(h, k)] = packed.tile([P, PER_ROUND, P], U32, name="codes", align_bytes=64)
+                scales[(h, k)] = packed.tile([P, PER_ROUND, P], U8, name="scales", align_bytes=64)
             nc.vector.quantize_mx(
-                out=codes[(h, k)][:].rearrange("p b m -> p (b m)").bitcast(FP8X4),
-                scales=scales[(h, k)][:].rearrange("p b m -> p (b m)"),
-                in_=grouped[(h, k)][:].rearrange("p b m t -> p (b m t)"),
+                out=codes[(h, k)][:, part].rearrange("p b m -> p (b m)").bitcast(FP8X4),
+                scales=scales[(h, k)][:, part].rearrange("p b m -> p (b m)"),
+                in_=grouped[(h, k)][:, part].rearrange("p b m t -> p (b m t)"),
             )
 
         def weigh_values(h, k):
-            for b, (i, r, c) in enumerate(PAIRS[k]):
-                if r % 2 == 0 and c == 0:
+            for b in range(PER_ROUND):
+                i, r, c = BANKS[PER_ROUND * k + b]
+                alone = (h, i) == (H - 1, CHUNKS - 1) and r >= 2
+                if c == 0 and (alone or r % 2 == 0):
                     ret["now"] = psum_ret.tile([P, 2, D], F32, name="ret_bank")
                 nc.tensor.matmul_mx(
                     out=ret["now"][:, r % 2, :],
                     lhsT=codes[(h, k)][:, b, :].bitcast(FP8X4),
                     lhsT_scale=scales[(h, k)][:, b, :],
-                    rhs=v_codes[(h, c)][:].bitcast(FP8X4),
-                    rhs_scale=v_scales[(h, c)][:],
+                    rhs=v_codes[h][:, c, :].bitcast(FP8X4),
+                    rhs_scale=v_scales[h][:, c, :],
                     start=(c == 0),
                     stop=(c == i),
                 )
-                if r % 2 == 1 and c == i:
+                if c == i and (alone or r % 2 == 1):
+                    first = r if alone else r - 1
+                    part = slice(first % 2, r % 2 + 1)
                     result = results.tile([P, 2, D], F32, name="result")
-                    nc.scalar.copy(out=result[:], in_=ret["now"][:])
+                    nc.scalar.copy(out=result[:, part], in_=ret["now"][:, part])
                     nc.sync.dma_start(
-                        out=out_rows[i, :, r - 1 : r + 1, h * D : (h + 1) * D], in_=result[:]
+                        out=out_rows[i, :, first : r + 1, h * D : (h + 1) * D], in_=result[:, part]
                     )
 
         load(0)
@@ -191,41 +209,42 @@ def tile_multiscaleretention_pb_kernel(tc, q_rot, k_scaled, v, out):
         for g in range(-1, last_round + MX_LAG + 1):
             h, k = divmod(g, ROUNDS)
             computing = 0 <= g <= last_round
-            first, second = PER_ROUND * k, PER_ROUND * k + 1
-            before = divmod(g - 1, ROUNDS)
             near = [(head, g - head * ROUNDS) for head in (h, h + 1) if 0 <= head < H]
             if computing and k == 0 and h + 2 < H:
                 load(h + 2)
             if computing:
-                scores(h, first, 0)
-                scores(h, first, 1)
+                scores(h, k, 0)
+                scores(h, k, 1)
             for head, step in near:
+                if (head, step) == (0, -1):
+                    turn_first()
+                    continue
                 for what, c in TURN_AT.get(step, ()):
                     turn(head, what, c)
             for head, step in near:
                 if step == DECAY_AT:
                     make_decay(head)
             if computing:
-                apply_decay(h, first, 0)
-            if 1 <= g <= last_round + 1:
-                quantise(before[0], PER_ROUND * before[1] + 1)
+                apply_decay(h, k, 0)
+                apply_decay(h, k, 1)
+            if 1 <= g <= last_round:
+                quantise(*divmod(g - 1, ROUNDS), slice(0, PER_ROUND))
             if computing:
-                apply_decay(h, first, 1)
-                scores(h, second, 0)
-                scores(h, second, 1)
-                apply_decay(h, second, 0)
+                scores(h, k, 2)
+                scores(h, k, 3)
+                apply_decay(h, k, 2)
             for head, step in near:
-                for c in range(CHUNKS):
-                    if step == REGROUP_AT[c] + 1:
-                        quantise_values(head, c)
+                if step == QUANTISE_VALUES_AT:
+                    quantise_values(head)
+            if g == last_round:
+                quantise(h, k, slice(0, 2))
             if computing:
-                quantise(h, first)
-                apply_decay(h, second, 1)
+                apply_decay(h, k, 3)
+            if g == last_round:
+                quantise(h, k, slice(2, 4))
             for head, step in near:
                 for c in range(CHUNKS):
                     if step == REGROUP_AT[c]:
                         regroup_values(head, c)
             if g >= MX_LAG:
-                h_due, k_due = divmod(g - MX_LAG, ROUNDS)
-                for k_in_round in range(PER_ROUND):
-                    weigh_values(h_due, PER_ROUND * k_due + k_in_round)
+                weigh_values(*divmod(g - MX_LAG, ROUNDS))

@@ -21,12 +21,8 @@ CHUNKS = N // CHUNK
 
 BANKS = [(i, r, c) for i in range(CHUNKS) for r in range(PACK) for c in range(i + 1)]
 PER_ROUND = 4
-MX_LAG = 2
 ROUNDS = len(BANKS) // PER_ROUND
-DECAY_AT = -1
-TURN_AT = {-1: (("k", 0), ("q", 0)), 0: (("q", 1), ("k", 1))}
-REGROUP_AT = [-1, 0]
-QUANTISE_VALUES_AT = 1
+BEFORE_LOADS, BEFORE_SCORES = 4, 2
 FAR = 1.0e6
 SPAN = N + PACK
 NEAR, FAR_OFF = slice(0, CHUNK + PACK), slice(CHUNK + PACK, SPAN)
@@ -49,12 +45,19 @@ def tile_multiscaleretention_pb_kernel(tc, q_rot, k_scaled, v, out):
         turned_pool = ctx.enter_context(tc.tile_pool(name="turned_pool", bufs=2))
         decays = ctx.enter_context(tc.tile_pool(name="decays", bufs=2))
         values_in = ctx.enter_context(tc.tile_pool(name="values_in", bufs=2))
-        packed = ctx.enter_context(tc.tile_pool(name="packed", bufs=4))
+        packed = ctx.enter_context(tc.tile_pool(name="packed", bufs=6))
         results = ctx.enter_context(tc.tile_pool(name="results", bufs=4))
-        psum_turn = ctx.enter_context(tc.psum_pool(name="psum_turn", bufs=2))
         psum_sim = ctx.enter_context(tc.psum_pool(name="psum_sim", bufs=4))
-        psum_ret = ctx.enter_context(tc.psum_pool(name="psum_ret", bufs=2))
+        psum_rest = ctx.enter_context(tc.psum_pool(name="psum_rest", bufs=4))
         ctx.enter_context(tc.manual_schedule())
+
+        zeros = const.tile([P, CHUNK], BF16)
+        nc.vector.memset(zeros[:], 0.0)
+        unread = psum_rest.tile([P, CHUNK], F32, name="bank")
+
+        def warm_up(count):
+            for n in range(count):
+                nc.tensor.matmul(unread[:], lhsT=zeros[:, 0:P], rhs=zeros[:], start=True, stop=True)
 
         identity = const.tile([P, P], F32)
         make_identity(nc, identity[:])
@@ -94,7 +97,7 @@ def tile_multiscaleretention_pb_kernel(tc, q_rot, k_scaled, v, out):
                 for part in halves:
                     nc.sync.dma_start(out=raws[(h, what)][:, c, part], in_=rows[:, part])
 
-        def turn(h, what, c, sets=range(PACK), bank_pool=psum_turn, copy=nc.scalar.copy):
+        def turn(h, what, c, sets=range(PACK), bank_pool=psum_rest, copy=nc.scalar.copy):
             if (h, what) not in turned:
                 turned[(h, what)] = turned_pool.tile(
                     [P, CHUNKS, PACK, P, PAIR], BF16, name=what + "_turned"
@@ -110,10 +113,12 @@ def tile_multiscaleretention_pb_kernel(tc, q_rot, k_scaled, v, out):
 
         def turn_first():
             low, high = range(0, 2), range(2, 4)
+            warm_up(BEFORE_LOADS)
             turn(0, "q", 0, low, psum_sim, nc.vector.tensor_copy)
-            turn(0, "k", 0, low, psum_turn, nc.scalar.copy)
-            turn(0, "k", 0, high, psum_turn, nc.vector.tensor_copy)
+            turn(0, "k", 0, low, psum_rest, nc.scalar.copy)
+            turn(0, "k", 0, high, psum_rest, nc.vector.tensor_copy)
             turn(0, "q", 0, high, psum_sim, nc.scalar.copy)
+            warm_up(BEFORE_SCORES)
 
         def make_decay(h):
             decay[h] = decays.tile([P, SPAN], F32, name="decay")
@@ -184,7 +189,7 @@ def tile_multiscaleretention_pb_kernel(tc, q_rot, k_scaled, v, out):
                 i, r, c = BANKS[PER_ROUND * k + b]
                 alone = (h, i) == (H - 1, CHUNKS - 1) and r >= 2
                 if c == 0 and (alone or r % 2 == 0):
-                    ret["now"] = psum_ret.tile([P, 2, D], F32, name="ret_bank")
+                    ret["now"] = psum_rest.tile([P, 2, D], F32, name="bank")
                 nc.tensor.matmul_mx(
                     out=ret["now"][:, r % 2, :],
                     lhsT=codes[(h, k)][:, b, :].bitcast(FP8X4),
@@ -198,53 +203,55 @@ def tile_multiscaleretention_pb_kernel(tc, q_rot, k_scaled, v, out):
                     first = r if alone else r - 1
                     part = slice(first % 2, r % 2 + 1)
                     result = results.tile([P, 2, D], F32, name="result")
-                    nc.scalar.copy(out=result[:, part], in_=ret["now"][:, part])
+                    copy = nc.vector.tensor_copy if alone and r == PACK - 1 else nc.scalar.copy
+                    copy(out=result[:, part], in_=ret["now"][:, part])
                     nc.sync.dma_start(
                         out=out_rows[i, :, first : r + 1, h * D : (h + 1) * D], in_=result[:, part]
                     )
 
         load(0)
         load(1)
-        last_round = H * ROUNDS - 1
-        for g in range(-1, last_round + MX_LAG + 1):
-            h, k = divmod(g, ROUNDS)
-            computing = 0 <= g <= last_round
-            near = [(head, g - head * ROUNDS) for head in (h, h + 1) if 0 <= head < H]
-            if computing and k == 0 and h + 2 < H:
-                load(h + 2)
-            if computing:
-                scores(h, k, 0)
-                scores(h, k, 1)
-            for head, step in near:
-                if (head, step) == (0, -1):
-                    turn_first()
-                    continue
-                for what, c in TURN_AT.get(step, ()):
-                    turn(head, what, c)
-            for head, step in near:
-                if step == DECAY_AT:
-                    make_decay(head)
-            if computing:
-                apply_decay(h, k, 0)
-                apply_decay(h, k, 1)
-            if 1 <= g <= last_round:
-                quantise(*divmod(g - 1, ROUNDS), slice(0, PER_ROUND))
-            if computing:
+        turn_first()
+        make_decay(0)
+        for h in range(H):
+            last_head = h == H - 1
+            for k in range(ROUNDS):
+                last_round = last_head and k == ROUNDS - 1
+                if k == 0 and h + 2 < H:
+                    load(h + 2)
+                for b in (0, 1):
+                    scores(h, k, b)
+                    apply_decay(h, k, b)
+                if (h, k) != (0, 0):
+                    quantise(*divmod(ROUNDS * h + k - 1, ROUNDS), slice(0, PER_ROUND))
+                if k == 0:
+                    regroup_values(h, 0)
+                    if h == 0:
+                        turn(0, "q", 1)
+                        turn(0, "k", 1)
+                    else:
+                        weigh_values(h - 1, 0)
+                    regroup_values(h, 1)
+                elif k == 1:
+                    quantise_values(h)
+                    if not last_head:
+                        make_decay(h + 1)
+                    if h > 0:
+                        weigh_values(h - 1, 1)
+                        weigh_values(h - 1, 2)
+                elif last_head:
+                    weigh_values(h, 0)
+                else:
+                    for what, c in (("k", 0), ("q", 0), ("q", 1), ("k", 1)):
+                        turn(h + 1, what, c)
                 scores(h, k, 2)
-                scores(h, k, 3)
                 apply_decay(h, k, 2)
-            for head, step in near:
-                if step == QUANTISE_VALUES_AT:
-                    quantise_values(head)
-            if g == last_round:
-                quantise(h, k, slice(0, 2))
-            if computing:
+                if last_round:
+                    quantise(h, k, slice(0, 2))
+                    quantise(h, k, slice(2, 3))
+                scores(h, k, 3)
                 apply_decay(h, k, 3)
-            if g == last_round:
-                quantise(h, k, slice(2, 4))
-            for head, step in near:
-                for c in range(CHUNKS):
-                    if step == REGROUP_AT[c]:
-                        regroup_values(head, c)
-            if g >= MX_LAG:
-                weigh_values(*divmod(g - MX_LAG, ROUNDS))
+                if last_round:
+                    quantise(h, k, slice(3, 4))
+        weigh_values(H - 1, 1)
+        weigh_values(H - 1, 2)

@@ -22,7 +22,7 @@ CHUNKS = N // CHUNK
 BANKS = [(i, r, c) for i in range(CHUNKS) for r in range(PACK) for c in range(i + 1)]
 PER_ROUND = 4
 ROUNDS = len(BANKS) // PER_ROUND
-BEFORE_LOADS, BEFORE_SCORES = 4, 2
+BEFORE_LOADS, BEFORE_SCORES = 14, 4
 FAR = 1.0e6
 SPAN = N + PACK
 NEAR, FAR_OFF = slice(0, CHUNK + PACK), slice(CHUNK + PACK, SPAN)
@@ -51,13 +51,13 @@ def tile_multiscaleretention_pb_kernel(tc, q_rot, k_scaled, v, out):
         psum_rest = ctx.enter_context(tc.psum_pool(name="psum_rest", bufs=4))
         ctx.enter_context(tc.manual_schedule())
 
-        zeros = const.tile([P, CHUNK], BF16)
+        zeros = const.tile([P, P], BF16)
         nc.vector.memset(zeros[:], 0.0)
-        unread = psum_rest.tile([P, CHUNK], F32, name="bank")
+        unread = psum_rest.tile([P, P], F32, name="bank")
 
         def warm_up(count):
             for n in range(count):
-                nc.tensor.matmul(unread[:], lhsT=zeros[:, 0:P], rhs=zeros[:], start=True, stop=True)
+                nc.tensor.matmul(unread[:], lhsT=zeros[:], rhs=zeros[:], start=True, stop=True)
 
         identity = const.tile([P, P], F32)
         make_identity(nc, identity[:])
@@ -90,26 +90,37 @@ def tile_multiscaleretention_pb_kernel(tc, q_rot, k_scaled, v, out):
             sources = {"q": q_rot, "k": k_scaled, "v": v}
             for what in ("q", "k", "v"):
                 raws[(h, what)] = raw.tile([P, CHUNKS, PACK, D], BF16, name=what + "_raw")
-            for what, c in (("q", 0), ("k", 0), ("v", 0), ("q", 1), ("k", 1), ("v", 1)):
+            whole, low, high = slice(0, PACK), slice(0, 2), slice(2, PACK)
+            pieces = [("k", 0, whole), ("q", 0, whole)]
+            if h == 0:
+                pieces = [("q", 0, low), ("k", 0, low), ("k", 0, high), ("q", 0, high)]
+            pieces += [("v", 0, whole), ("q", 1, whole), ("k", 1, whole), ("v", 1, whole)]
+            for what, c, part in pieces:
                 rows = sources[what][0, h, c * CHUNK : (c + 1) * CHUNK, :]
                 rows = rows.rearrange("(p t) d -> p t d", t=PACK)
-                halves = (slice(0, 2), slice(2, 4)) if (h, c) == (0, 0) and what != "v" else (slice(0, 4),)
-                for part in halves:
-                    nc.sync.dma_start(out=raws[(h, what)][:, c, part], in_=rows[:, part])
+                nc.sync.dma_start(out=raws[(h, what)][:, c, part], in_=rows[:, part])
 
         def turn(h, what, c, sets=range(PACK), bank_pool=psum_rest, copy=nc.scalar.copy):
             if (h, what) not in turned:
-                turned[(h, what)] = turned_pool.tile(
-                    [P, CHUNKS, PACK, P, PAIR], BF16, name=what + "_turned"
-                )
+                shape = [P, CHUNKS, PACK, P, PAIR] if what == "k" else [P, CHUNKS, PAIR, PACK, P]
+                turned[(h, what)] = turned_pool.tile(shape, BF16, name=what + "_turned")
             bank = bank_pool.tile([P, PACK, P], F32, name="bank")
             for t in sets:
                 nc.tensor.transpose(
                     bank[:, t, :], raws[(h, what)][:, c, t, :].bitcast(F32), identity[:]
                 )
             part = slice(sets[0], sets[-1] + 1)
-            words = turned[(h, what)][:, c, part].rearrange("w t p e -> w (t p e)").bitcast(F32)
-            copy(out=words, in_=bank[:, part].rearrange("w t p -> w (t p)"))
+            words = bank[:, part].rearrange("w t p -> w (t p)")
+            if what == "k":
+                copy(
+                    out=turned[(h, what)][:, c, part].rearrange("w t p e -> w (t p e)").bitcast(F32),
+                    in_=words,
+                )
+            else:
+                copy(
+                    out=turned[(h, what)][:, c, :, part].rearrange("w e t p -> w e (t p)"),
+                    in_=words.bitcast(BF16).rearrange("w (x e) -> w e x", e=PAIR),
+                )
 
         def turn_first():
             low, high = range(0, 2), range(2, 4)
@@ -156,7 +167,7 @@ def tile_multiscaleretention_pb_kernel(tc, q_rot, k_scaled, v, out):
                     nc.tensor.matmul(
                         sums[:, t, :],
                         lhsT=turned[(h, "k")][:, c, t, :, e],
-                        rhs=turned[(h, "q")][:, i, r, :, e],
+                        rhs=turned[(h, "q")][:, i, e, r, :],
                         start=(e == 0),
                         stop=(e == PAIR - 1),
                     )

import math
from contextlib import ExitStack

import concourse.mybir as mybir
from concourse.masks import make_identity

BF16 = mybir.dt.bfloat16
F32 = mybir.dt.float32
U32 = mybir.dt.uint32
U8 = mybir.dt.uint8
FP8X4 = mybir.dt.float8_e4m3fn_x4

H = 8
N = 1024
D = 256
P = 128
PACK = 4
PAIR = 2
CHUNK = PACK * P
CHUNKS = N // CHUNK

BANKS = [(i, r, c) for i in range(CHUNKS) for r in range(PACK) for c in range(i + 1)]
PER_ROUND = 4
ROUNDS = len(BANKS) // PER_ROUND
BEFORE_LOADS, BEFORE_SCORES = 14, 4
FAR = 1.0e6
SPAN = N + PACK
NEAR, FAR_OFF = slice(0, CHUNK + PACK), slice(CHUNK + PACK, SPAN)

FLOPS = 2 * 2 * H * D * len(BANKS) * P * CHUNK


def log_decay(h):
    first, last = math.log(2.0 ** -5), math.log(2.0 ** -9)
    return math.log(1.0 - math.exp(first + (last - first) * h / (H - 1)))


def tile_multiscaleretention_pb_kernel(tc, q_rot, k_scaled, v, out):
    nc = tc.nc
    out_rows = out[0].rearrange("(i p r) e -> i p r e", p=P, r=PACK)

    with ExitStack() as ctx:
        const = ctx.enter_context(tc.tile_pool(name="const", bufs=1))
        raw = ctx.enter_context(tc.tile_pool(name="raw", bufs=3))
        turned_pool = ctx.enter_context(tc.tile_pool(name="turned_pool", bufs=2))
        decays = ctx.enter_context(tc.tile_pool(name="decays", bufs=2))
        values_in = ctx.enter_context(tc.tile_pool(name="values_in", bufs=2))
        packed = ctx.enter_context(tc.tile_pool(name="packed", bufs=6))
        results = ctx.enter_context(tc.tile_pool(name="results", bufs=4))
        psum_sim = ctx.enter_context(tc.psum_pool(name="psum_sim", bufs=4))
        psum_rest = ctx.enter_context(tc.psum_pool(name="psum_rest", bufs=4))
        ctx.enter_context(tc.manual_schedule())

        zeros = const.tile([P, P], BF16)
        nc.vector.memset(zeros[:], 0.0)
        unread = psum_rest.tile([P, P], F32, name="bank")

        def warm_up(count):
            for n in range(count):
                nc.tensor.matmul(unread[:], lhsT=zeros[:], rhs=zeros[:], start=True, stop=True)

        identity = const.tile([P, P], F32)
        make_identity(nc, identity[:])
        distance = const.tile([P, SPAN], F32)
        for part in (NEAR, FAR_OFF):
            nc.gpsimd.iota(
                distance[:, part], pattern=[[1, part.stop - part.start]],
                base=part.start - (PACK - 1), channel_multiplier=-PACK,
                allow_small_or_imprecise_dtypes=True,
            )
        near_part = distance[:, 0:CHUNK]
        nc.vector.scalar_tensor_tensor(
            out=near_part,
            in0=near_part,
            scalar=-FAR,
            in1=near_part,
            op0=mybir.AluOpType.mult,
            op1=mybir.AluOpType.max,
        )

        raws = {}
        turned = {}
        decay = {}
        v_grouped, v_codes, v_scales = {}, {}, {}
        sim = {}
        grouped, codes, scales = {}, {}, {}
        ret = {}

        def load(h):
            sources = {"q": q_rot, "k": k_scaled, "v": v}
            for what in ("q", "k", "v"):
                raws[(h, what)] = raw.tile([P, CHUNKS, PACK, D], BF16, name=what + "_raw")
            whole, low, high = slice(0, PACK), slice(0, 2), slice(2, PACK)
            pieces = [("k", 0, whole), ("q", 0, whole)]
            if h == 0:
                pieces = [("q", 0, low), ("k", 0, low), ("k", 0, high), ("q", 0, high)]
            pieces += [("v", 0, whole), ("q", 1, whole), ("k", 1, whole), ("v", 1, whole)]
            for what, c, part in pieces:
                rows = sources[what][0, h, c * CHUNK : (c + 1) * CHUNK, :]
                rows = rows.rearrange("(p t) d -> p t d", t=PACK)
                nc.sync.dma_start(out=raws[(h, what)][:, c, part], in_=rows[:, part])

        def turn(h, what, c, sets=range(PACK), bank_pool=psum_rest, copy=nc.scalar.copy):
            if (h, what) not in turned:
                shape = [P, CHUNKS, PACK, P, PAIR] if what == "k" else [P, CHUNKS, PAIR, PACK, P]
                turned[(h, what)] = turned_pool.tile(shape, BF16, name=what + "_turned")
            bank = bank_pool.tile([P, PACK, P], F32, name="bank")
            for t in sets:
                nc.tensor.transpose(
                    bank[:, t, :], raws[(h, what)][:, c, t, :].bitcast(F32), identity[:]
                )
            part = slice(sets[0], sets[-1] + 1)
            words = bank[:, part].rearrange("w t p -> w (t p)")
            if what == "k":
                copy(
                    out=turned[(h, what)][:, c, part].rearrange("w t p e -> w (t p e)").bitcast(F32),
                    in_=words,
                )
            else:
                copy(
                    out=turned[(h, what)][:, c, :, part].rearrange("w e t p -> w e (t p)"),
                    in_=words.bitcast(BF16).rearrange("w (x e) -> w e x", e=PAIR),
                )

        def turn_first():
            low, high = range(0, 2), range(2, 4)
            warm_up(BEFORE_LOADS)
            turn(0, "q", 0, low, psum_sim, nc.vector.tensor_copy)
            turn(0, "k", 0, low, psum_rest, nc.scalar.copy)
            turn(0, "k", 0, high, psum_rest, nc.vector.tensor_copy)
            turn(0, "q", 0, high, psum_sim, nc.scalar.copy)
            warm_up(BEFORE_SCORES)

        def make_decay(h):
            decay[h] = decays.tile([P, SPAN], F32, name="decay")
            for part in (NEAR, FAR_OFF) if h == 0 else (slice(0, SPAN),):
                nc.scalar.activation(
                    out=decay[h][:, part],
                    in_=distance[:, part],
                    func=mybir.ActivationFunctionType.Exp,
                    scale=log_decay(h),
                )

        def regroup_values(h, c):
            if c == 0:
                v_grouped[h] = values_in.tile([P, CHUNKS, D, PACK], BF16, name="v_grouped", align_bytes=64)
            nc.scalar.copy(
                out=v_grouped[h][:, c].rearrange("p (b i) t -> p b t i", i=4),
                in_=raws[(h, "v")][:, c].rearrange("p t (b i) -> p b t i", i=4),
            )

        def quantise_values(h):
            v_codes[h] = values_in.tile([P, CHUNKS, D], U32, name="v_codes", align_bytes=64)
            v_scales[h] = values_in.tile([P, CHUNKS, D], U8, name="v_scales", align_bytes=64)
            nc.vector.quantize_mx(
                out=v_codes[h][:].rearrange("p c d -> p (c d)").bitcast(FP8X4),
                scales=v_scales[h][:].rearrange("p c d -> p (c d)"),
                in_=v_grouped[h][:].rearrange("p c d t -> p (c d t)"),
            )

        def scores(h, k, b):
            i, r, c = BANKS[PER_ROUND * k + b]
            sums = psum_sim.tile([P, PACK, P], F32, name="bank")
            sim[(h, k, b)] = sums
            for t in range(PACK):
                for e in range(PAIR):
                    nc.tensor.matmul(
                        sums[:, t, :],
                        lhsT=turned[(h, "k")][:, c, t, :, e],
                        rhs=turned[(h, "q")][:, i, e, r, :],
                        start=(e == 0),
                        stop=(e == PAIR - 1),
                    )

        def apply_decay(h, k, b):
            i, r, c = BANKS[PER_ROUND * k + b]
            if b == 0:
                grouped[(h, k)] = packed.tile([P, PER_ROUND, P, PACK], BF16, name="grouped", align_bytes=64)
            first = CHUNK * (i - c) + r
            window = decay[h][:, first : first + CHUNK].rearrange("p (m z) -> p m z", z=PACK)
            nc.vector.tensor_tensor(
                out=grouped[(h, k)][:, b],
                in0=sim[(h, k, b)][:].rearrange("p t m -> p m t"),
                in1=window[:, :, ::-1],
                op=mybir.AluOpType.mult,
            )

        def quantise(h, k, part):
            if part.start == 0:
                codes[(h, k)] = packed.tile([P, PER_ROUND, P], U32, name="codes", align_bytes=64)
                scales[(h, k)] = packed.tile([P, PER_ROUND, P], U8, name="scales", align_bytes=64)
            nc.vector.quantize_mx(
                out=codes[(h, k)][:, part].rearrange("p b m -> p (b m)").bitcast(FP8X4),
                scales=scales[(h, k)][:, part].rearrange("p b m -> p (b m)"),
                in_=grouped[(h, k)][:, part].rearrange("p b m t -> p (b m t)"),
            )

        def weigh_values(h, k):
            for b in range(PER_ROUND):
                i, r, c = BANKS[PER_ROUND * k + b]
                alone = (h, i) == (H - 1, CHUNKS - 1) and r >= 2
                if c == 0 and (alone or r % 2 == 0):
                    ret["now"] = psum_rest.tile([P, 2, D], F32, name="bank")
                nc.tensor.matmul_mx(
                    out=ret["now"][:, r % 2, :],
                    lhsT=codes[(h, k)][:, b, :].bitcast(FP8X4),
                    lhsT_scale=scales[(h, k)][:, b, :],
                    rhs=v_codes[h][:, c, :].bitcast(FP8X4),
                    rhs_scale=v_scales[h][:, c, :],
                    start=(c == 0),
                    stop=(c == i),
                )
                if c == i and (alone or r % 2 == 1):
                    first = r if alone else r - 1
                    part = slice(first % 2, r % 2 + 1)
                    result = results.tile([P, 2, D], F32, name="result")
                    copy = nc.vector.tensor_copy if alone and r == PACK - 1 else nc.scalar.copy
                    copy(out=result[:, part], in_=ret["now"][:, part])
                    nc.sync.dma_start(
                        out=out_rows[i, :, first : r + 1, h * D : (h + 1) * D], in_=result[:, part]
                    )

        load(0)
        load(1)
        turn_first()
        make_decay(0)
        for h in range(H):
            last_head = h == H - 1
            for k in range(ROUNDS):
                last_round = last_head and k == ROUNDS - 1
                if k == 0 and h + 2 < H:
                    load(h + 2)
                for b in (0, 1):
                    scores(h, k, b)
                    apply_decay(h, k, b)
                if (h, k) != (0, 0):
                    quantise(*divmod(ROUNDS * h + k - 1, ROUNDS), slice(0, PER_ROUND))
                if k == 0:
                    regroup_values(h, 0)
                    if h == 0:
                        turn(0, "q", 1)
                        turn(0, "k", 1)
                    else:
                        weigh_values(h - 1, 0)
                    regroup_values(h, 1)
                elif k == 1:
                    quantise_values(h)
                    if not last_head:
                        make_decay(h + 1)
                    if h > 0:
                        weigh_values(h - 1, 1)
                        weigh_values(h - 1, 2)
                elif last_head:
                    weigh_values(h, 0)
                else:
                    for what, c in (("k", 0), ("q", 0), ("q", 1), ("k", 1)):
                        turn(h + 1, what, c)
                scores(h, k, 2)
                apply_decay(h, k, 2)
                if last_round:
                    quantise(h, k, slice(0, 2))
                    quantise(h, k, slice(2, 3))
                scores(h, k, 3)
                apply_decay(h, k, 3)
                if last_round:
                    quantise(h, k, slice(3, 4))
        weigh_values(H - 1, 1)
        weigh_values(H - 1, 2)
